import numpy as np
import ml_dtypes


def mxq(x, axis, fmt="e4m3"):
    dtype, down = {"e4m3": (ml_dtypes.float8_e4m3fn, 7), "e5m2": (ml_dtypes.float8_e5m2, 14)}[fmt]
    v = np.moveaxis(np.asarray(x, np.float32).astype(ml_dtypes.bfloat16).astype(np.float64), axis, -1)
    blocks = v.reshape(v.shape[:-1] + (-1, 32))
    amax = np.abs(blocks).max(-1, keepdims=True)
    byte = np.maximum(np.where(amax > 0, np.frexp(amax)[1] - 1 + 127, 0) - down, 1)
    scale = np.exp2(byte - 127.0)
    codes = (blocks / scale).astype(np.float32).astype(dtype).astype(np.float64)
    return np.moveaxis((codes * scale).reshape(v.shape), -1, axis)


WIDE = False


def mx_kscale(k):
    if not WIDE:
        return np.ones(k)
    levels = np.array([10, -10, 5, -5, 0])
    a = np.random.permutation(np.resize(levels, k // 512 * 4)).reshape(k // 512, 4)
    idx = np.arange(k)
    return np.exp2(a[idx // 512, idx % 128 // 32])


BF16 = ml_dtypes.bfloat16


def bf(x):
    return np.asarray(x, np.float32).astype(BF16)


def f64(x):
    return np.asarray(x).astype(np.float64)


B, N, NF, ND, NH = 4, 32, 512, 1024, 512


def setup_inputs():
    s = mx_kscale(ND)
    t = mx_kscale(NH)
    return {
        "atom_features": bf(np.random.standard_normal((B, N, NF))),
        "distance_matrix": bf(np.random.random((B, N, N, ND)) * s),
        "distance_matrix_mask": bf(0.25 + 0.75 * np.random.random((B, N, N))),
        "W_cf": bf(np.random.standard_normal((NF, NH)) / np.sqrt(NF) * t),
        "W_df": bf(np.random.standard_normal((ND, NH)) * 1.5 / np.sqrt(ND) / s[:, None]),
        "W_fc": bf(np.random.standard_normal((NH, NF)) / np.sqrt(NH) / t[:, None]),
        "b_cf": bf(np.random.standard_normal(NH) * 0.3 * t),
        "b_df": bf(np.random.standard_normal(NH) * 0.3),
    }


def reference(atom_features, distance_matrix, distance_matrix_mask, W_cf, W_df, W_fc, b_cf, b_df):
    a = f64(atom_features)
    dist_h = (mxq(f64(distance_matrix), 3, "e4m3") @ mxq(f64(W_df), 0, "e4m3")) + f64(b_df)
    atom_h = a @ f64(W_cf) + f64(b_cf)
    gated = dist_h * atom_h[:, None, :, :]
    out = mxq(gated, 3, "e4m3") @ mxq(f64(W_fc), 0, "e4m3")
    out = out * f64(distance_matrix_mask)[..., None]
    return np.tanh(out).sum(axis=2) + a

@@ -1,0 +1,271 @@
+from contextlib import ExitStack
+
+import concourse.mybir as mybir
+from concourse.masks import make_identity
+
+F32 = mybir.dt.float32
+BF16 = mybir.dt.bfloat16
+U32 = mybir.dt.uint32
+U8 = mybir.dt.uint8
+FP8X4 = mybir.dt.float8_e4m3fn_x4
+FUNC = mybir.ActivationFunctionType
+ALU = mybir.AluOpType
+
+P = 128
+PACK = 4
+K_PASS = P * PACK
+
+MOLS, ATOMS = 4, 32
+NF, ND, NH = 512, 1024, 512
+assert MOLS * ATOMS == P and NH == K_PASS
+
+D_PASSES = ND // K_PASS
+F_CHUNKS = NF // P
+TILES = 2
+ROUNDS = ATOMS // TILES
+COLS = TILES * P
+RUN = 4
+
+FLOPS = 2 * (MOLS * ATOMS * ATOMS * (ND * NH + NH * NF) + MOLS * ATOMS * NF * NH)
+
+
+def regroup(copy, grouped, rows):
+    copy(
+        out=grouped.rearrange("p (c i t) -> p c t i", i=RUN, t=PACK),
+        in_=rows.rearrange("p t (c i) -> p c t i", i=RUN),
+    )
+
+
+def tile_dtnnstep_pa_kernel(
+    tc, atom_features, distance_matrix, distance_matrix_mask, W_cf, W_df, W_fc, b_cf, b_df, out
+):
+    nc = tc.nc
+    with ExitStack() as ctx:
+        keep = ctx.enter_context(tc.tile_pool(name="keep", bufs=1))
+        ring = ctx.enter_context(tc.tile_pool(name="ring", bufs=2))
+        tanh_pool = ctx.enter_context(tc.tile_pool(name="tanh_pool", bufs=2 * TILES))
+        psum_flip = ctx.enter_context(tc.psum_pool(name="psum_flip", bufs=2))
+        psum_dist = ctx.enter_context(tc.psum_pool(name="psum_dist", bufs=4))
+        psum_pair = ctx.enter_context(tc.psum_pool(name="psum_pair", bufs=2))
+        ctx.enter_context(tc.manual_schedule())
+
+        wdf_raw = keep.tile([P, D_PASSES, PACK, NH], BF16, name="wdf_raw")
+        for g in range(D_PASSES):
+            nc.sync.dma_start(
+                out=wdf_raw[:, g, :, :].rearrange("q (u e) h -> q u (e h)", e=2),
+                in_=W_df[g * K_PASS : (g + 1) * K_PASS, :].rearrange(
+                    "(u q e) h -> q u (e h)", q=P, e=2
+                ),
+            )
+
+        d_rows = distance_matrix.rearrange("b i j k -> (b i) j k")
+        d_sb = [keep.tile([P, TILES, ND], BF16, name="d%d" % n) for n in range(ROUNDS)]
+
+        def load_distances(n):
+            nc.sync.dma_start(out=d_sb[n][:], in_=d_rows[:, n * TILES : (n + 1) * TILES, :])
+
+        load_distances(0)
+        wcf_sb = keep.tile([P, F_CHUNKS, NH], BF16, name="wcf_sb")
+        nc.sync.dma_start(out=wcf_sb[:], in_=W_cf.rearrange("(c p) h -> p c h", p=P))
+        wfc_raw = keep.tile([P, PACK, NF], BF16, name="wfc_raw")
+        nc.sync.dma_start(out=wfc_raw[:], in_=W_fc.rearrange("(p t) f -> p t f", t=PACK))
+        for n in range(1, ROUNDS):
+            load_distances(n)
+
+        a_sb = keep.tile([P, NF], BF16, name="a_sb")
+        nc.scalar.dma_start(out=a_sb[:], in_=atom_features.rearrange("b n f -> (b n) f"))
+        bcf_bf = keep.tile([P, PACK], BF16, name="bcf_bf")
+        nc.scalar.dma_start(out=bcf_bf[:], in_=b_cf.rearrange("(p t) -> p t", t=PACK))
+        bdf_bf = keep.tile([P, PACK], BF16, name="bdf_bf")
+        nc.scalar.dma_start(out=bdf_bf[:], in_=b_df.rearrange("(p t) -> p t", t=PACK))
+        mask_bf = keep.tile([P, ATOMS], BF16, name="mask_bf")
+        nc.scalar.dma_start(out=mask_bf[:], in_=distance_matrix_mask.rearrange("b i j -> (b i) j"))
+
+        ident_f32 = keep.tile([P, P], F32, name="ident_f32")
+        make_identity(nc, ident_f32[:])
+        ident_bf = keep.tile([P, P], BF16, name="ident_bf")
+        make_identity(nc, ident_bf[:])
+
+        bcf = keep.tile([P, PACK], F32, name="bcf")
+        nc.vector.tensor_copy(out=bcf[:], in_=bcf_bf[:])
+        bdf = keep.tile([P, PACK], F32, name="bdf")
+        nc.vector.tensor_copy(out=bdf[:], in_=bdf_bf[:])
+        mask = keep.tile([P, ATOMS], F32, name="mask")
+        nc.vector.tensor_copy(out=mask[:], in_=mask_bf[:])
+
+        wdf_grouped = keep.tile([P, D_PASSES, NH * PACK], BF16, name="wdf_grouped", align_bytes=64)
+        wdf_codes = keep.tile([P, D_PASSES, NH], U32, name="wdf_codes", align_bytes=64)
+        wdf_scales = keep.tile([P, D_PASSES, NH], U8, name="wdf_scales", align_bytes=64)
+        for g in range(D_PASSES):
+            nc.vector.tensor_copy(
+                out=wdf_grouped[:, g, :].rearrange("p (t q v) -> p t q v", t=PACK, v=PACK),
+                in_=wdf_raw[:, g, :, :].rearrange("p v (q t) -> p t q v", t=PACK),
+            )
+        for g in range(D_PASSES):
+            nc.vector.quantize_mx(
+                out=wdf_codes[:, g, :].bitcast(FP8X4),
+                scales=wdf_scales[:, g, :],
+                in_=wdf_grouped[:, g, :],
+            )
+
+        d_grouped, d_codes, d_scales, dist_banks = {}, {}, {}, {}
+        planar, g_grouped, g_codes, g_scales, tanh_tiles = {}, {}, {}, {}, {}
+
+        def transpose_distances(n):
+            d_grouped[n] = ring.tile(
+                [P, D_PASSES * COLS * PACK], BF16, name="d_grouped", align_bytes=64
+            )
+            grouped_words = (
+                d_grouped[n][:]
+                .bitcast(F32)
+                .rearrange("p (g a m u) -> p a g m u", g=D_PASSES, a=TILES, u=2)
+            )
+            for a in range(TILES):
+                words = d_sb[n][:, a, :].bitcast(F32)
+                flipped = psum_flip.tile([P, D_PASSES, 2, P], F32, name="flipped")
+                for g in range(D_PASSES):
+                    for u in range(2):
+                        first = (2 * g + u) * P
+                        nc.tensor.transpose(
+                            flipped[:, g, u, :], words[:, first : first + P], ident_f32[:]
+                        )
+                nc.scalar.copy(
+                    out=grouped_words[:, a, :, :, :],
+                    in_=flipped[:].rearrange("p g u m -> p g m u"),
+                )
+
+        def quantise_distances(n):
+            d_codes[n] = ring.tile([P, D_PASSES * COLS], U32, name="d_codes", align_bytes=64)
+            d_scales[n] = ring.tile([P, D_PASSES * COLS], U8, name="d_scales", align_bytes=64)
+            nc.vector.quantize_mx(
+                out=d_codes[n][:].bitcast(FP8X4), scales=d_scales[n][:], in_=d_grouped[n][:]
+            )
+
+        def first_product(n):
+            dist_banks[n] = []
+            for half in range(PACK // 2):
+                bank = psum_dist.tile([P, 2, COLS], F32, name="dist_bank")
+                dist_banks[n].append(bank)
+                for w in range(2):
+                    h_cols = slice((2 * half + w) * P, (2 * half + w + 1) * P)
+                    for g in range(D_PASSES):
+                        pairs = slice(g * COLS, (g + 1) * COLS)
+                        nc.tensor.matmul_mx(
+                            out=bank[:, w, :],
+                            lhsT=wdf_codes[:, g, h_cols].bitcast(FP8X4),
+                            lhsT_scale=wdf_scales[:, g, h_cols],
+                            rhs=d_codes[n][:, pairs].bitcast(FP8X4),
+                            rhs_scale=d_scales[n][:, pairs],
+                            start=(g == 0),
+                            stop=(g == D_PASSES - 1),
+                        )
+
+        def gate(n):
+            planar[n] = ring.tile([P, PACK, COLS], BF16, name="planar")
+            for t in range(PACK):
+                nc.vector.scalar_tensor_tensor(
+                    out=planar[n][:, t, :].rearrange("p (c i) -> p c i", i=ATOMS),
+                    in0=dist_banks[n][t // 2][:, t % 2, :].rearrange("p (c i) -> p c i", i=ATOMS),
+                    scalar=bdf[:, t : t + 1],
+                    in1=atom_gate[:, t, n * TILES * MOLS : (n + 1) * TILES * MOLS]
+                    .unsqueeze(2)
+                    .to_broadcast([P, TILES * MOLS, ATOMS]),
+                    op0=ALU.add,
+                    op1=ALU.mult,
+                )
+
+        def regroup_gated(n):
+            g_grouped[n] = ring.tile([P, COLS * PACK], BF16, name="g_grouped", align_bytes=64)
+            regroup(nc.scalar.copy, g_grouped[n][:], planar[n][:])
+
+        def quantise_gated(n):
+            g_codes[n] = ring.tile([P, COLS], U32, name="g_codes", align_bytes=64)
+            g_scales[n] = ring.tile([P, COLS], U8, name="g_scales", align_bytes=64)
+            nc.vector.quantize_mx(
+                out=g_codes[n][:].bitcast(FP8X4), scales=g_scales[n][:], in_=g_grouped[n][:]
+            )
+
+        def second_product(n):
+            tanh_tiles[n] = []
+            for a in range(TILES):
+                j = n * TILES + a
+                pairs = slice(a * P, (a + 1) * P)
+                product = psum_pair.tile([P, NF], F32, name="product")
+                nc.tensor.matmul_mx(
+                    out=product[:],
+                    lhsT=g_codes[n][:, pairs].bitcast(FP8X4),
+                    lhsT_scale=g_scales[n][:, pairs],
+                    rhs=wfc_codes[:].bitcast(FP8X4),
+                    rhs_scale=wfc_scales[:],
+                    start=True,
+                    stop=True,
+                )
+                squashed = tanh_pool.tile([P, NF], F32, name="squashed")
+                tanh_tiles[n].append(squashed)
+                nc.scalar.activation(
+                    out=squashed[:], in_=product[:], func=FUNC.Tanh, scale=mask[:, j : j + 1]
+                )
+
+        def add_to_sum(n):
+            for squashed in tanh_tiles[n]:
+                nc.vector.tensor_tensor(out=total[:], in0=total[:], in1=squashed[:], op=ALU.add)
+
+        aT_ps = psum_pair.tile([P, F_CHUNKS, P], BF16, name="aT_ps", tag="product")
+        for c in range(F_CHUNKS):
+            nc.tensor.transpose(aT_ps[:, c, :], a_sb[:, c * P : (c + 1) * P], ident_bf[:])
+        aT = keep.tile([P, F_CHUNKS, P], BF16, name="aT")
+        nc.scalar.copy(out=aT[:], in_=aT_ps[:])
+
+        transpose_distances(0)
+        quantise_distances(0)
+
+        atom_ps = psum_pair.tile([P, PACK, P], F32, name="atom_ps", tag="product")
+        wcf_cols = wcf_sb[:].rearrange("p c (q t) -> p c t q", t=PACK)
+        for t in range(PACK):
+            for c in range(F_CHUNKS):
+                nc.tensor.matmul(
+                    out=atom_ps[:, t, :],
+                    lhsT=wcf_cols[:, c, t, :],
+                    rhs=aT[:, c, :],
+                    start=(c == 0),
+                    stop=(c == F_CHUNKS - 1),
+                )
+        atom_gate = keep.tile([P, PACK, ATOMS * MOLS], F32, name="atom_gate")
+        for t in range(PACK):
+            nc.scalar.activation(
+                out=atom_gate[:, t, :].rearrange("p (j b) -> p j b", b=MOLS),
+                in_=atom_ps[:, t, :].rearrange("p (b j) -> p j b", b=MOLS),
+                func=FUNC.Identity,
+                bias=bcf[:, t : t + 1],
+            )
+
+        wfc_grouped = keep.tile([P, NF * PACK], BF16, name="wfc_grouped", align_bytes=64)
+        wfc_codes = keep.tile([P, NF], U32, name="wfc_codes", align_bytes=64)
+        wfc_scales = keep.tile([P, NF], U8, name="wfc_scales", align_bytes=64)
+        regroup(nc.vector.tensor_copy, wfc_grouped[:], wfc_raw[:])
+        total = keep.tile([P, NF], F32, name="total")
+        nc.vector.tensor_copy(out=total[:], in_=a_sb[:])
+        nc.vector.quantize_mx(
+            out=wfc_codes[:].bitcast(FP8X4), scales=wfc_scales[:], in_=wfc_grouped[:]
+        )
+
+        def live(n):
+            return 0 <= n < ROUNDS
+
+        for s in range(1, ROUNDS + 4):
+            if live(s):
+                transpose_distances(s)
+            if live(s - 4):
+                add_to_sum(s - 4)
+            if live(s - 1):
+                first_product(s - 1)
+                gate(s - 1)
+            if live(s):
+                quantise_distances(s)
+            if live(s - 2):
+                regroup_gated(s - 2)
+                quantise_gated(s - 2)
+            if live(s - 3):
+                second_product(s - 3)
+
+        nc.sync.dma_start(out=out.rearrange("b i f -> (b i) f"), in_=total[:])

@@ -42,11 +42,12 @@ def tile_dtnnstep_pa_kernel(
     nc = tc.nc
     with ExitStack() as ctx:
         keep = ctx.enter_context(tc.tile_pool(name="keep", bufs=1))
-        ring = ctx.enter_context(tc.tile_pool(name="ring", bufs=2))
-        tanh_pool = ctx.enter_context(tc.tile_pool(name="tanh_pool", bufs=2 * TILES))
+        ring = ctx.enter_context(tc.tile_pool(name="ring", bufs=3))
+        tanh_pool = ctx.enter_context(tc.tile_pool(name="tanh_pool", bufs=3 * TILES))
         psum_flip = ctx.enter_context(tc.psum_pool(name="psum_flip", bufs=2))
-        psum_dist = ctx.enter_context(tc.psum_pool(name="psum_dist", bufs=4))
+        psum_dist = ctx.enter_context(tc.psum_pool(name="psum_dist", bufs=3))
         psum_pair = ctx.enter_context(tc.psum_pool(name="psum_pair", bufs=2))
+        psum_sum = ctx.enter_context(tc.psum_pool(name="psum_sum", bufs=1))
         ctx.enter_context(tc.manual_schedule())
 
         wdf_raw = keep.tile([P, D_PASSES, PACK, NH], BF16, name="wdf_raw")
@@ -80,6 +81,10 @@ def tile_dtnnstep_pa_kernel(
         nc.scalar.dma_start(out=bdf_bf[:], in_=b_df.rearrange("(p t) -> p t", t=PACK))
         mask_bf = keep.tile([P, ATOMS], BF16, name="mask_bf")
         nc.scalar.dma_start(out=mask_bf[:], in_=distance_matrix_mask.rearrange("b i j -> (b i) j"))
+
+        warm = keep.tile([P, 1], F32, name="warm")
+        nc.vector.memset(warm[:], 0.0)
+        nc.scalar.activation(out=warm[:], in_=warm[:], func=FUNC.Tanh)
 
         ident_f32 = keep.tile([P, P], F32, name="ident_f32")
         make_identity(nc, ident_f32[:])
@@ -176,7 +181,7 @@ def tile_dtnnstep_pa_kernel(
 
         def regroup_gated(n):
             g_grouped[n] = ring.tile([P, COLS * PACK], BF16, name="g_grouped", align_bytes=64)
-            regroup(nc.scalar.copy, g_grouped[n][:], planar[n][:])
+            regroup(nc.vector.tensor_copy, g_grouped[n][:], planar[n][:])
 
         def quantise_gated(n):
             g_codes[n] = ring.tile([P, COLS], U32, name="g_codes", align_bytes=64)
@@ -207,14 +212,30 @@ def tile_dtnnstep_pa_kernel(
                 )
 
         def add_to_sum(n):
-            for squashed in tanh_tiles[n]:
-                nc.vector.tensor_tensor(out=total[:], in0=total[:], in1=squashed[:], op=ALU.add)
+            for a in range(TILES):
+                for c in range(F_CHUNKS):
+                    nc.tensor.matmul(
+                        out=sum_T[:, c, :],
+                        lhsT=tanh_tiles[n][a][:, c * P : (c + 1) * P],
+                        rhs=ident_f32[:],
+                        is_transpose=True,
+                        start=False,
+                        stop=(n == ROUNDS - 1 and a == TILES - 1 and c == F_CHUNKS - 1),
+                    )
 
         aT_ps = psum_pair.tile([P, F_CHUNKS, P], BF16, name="aT_ps", tag="product")
         for c in range(F_CHUNKS):
             nc.tensor.transpose(aT_ps[:, c, :], a_sb[:, c * P : (c + 1) * P], ident_bf[:])
         aT = keep.tile([P, F_CHUNKS, P], BF16, name="aT")
         nc.scalar.copy(out=aT[:], in_=aT_ps[:])
+        sum_T = psum_sum.tile([P, F_CHUNKS, P], F32, name="sum_T")
+        nc.tensor.matmul(
+            out=sum_T[:].rearrange("q c m -> q (c m)"),
+            lhsT=ident_bf[:],
+            rhs=aT[:].rearrange("q c m -> q (c m)"),
+            start=True,
+            stop=False,
+        )
 
         transpose_distances(0)
         quantise_distances(0)
@@ -243,8 +264,6 @@ def tile_dtnnstep_pa_kernel(
         wfc_codes = keep.tile([P, NF], U32, name="wfc_codes", align_bytes=64)
         wfc_scales = keep.tile([P, NF], U8, name="wfc_scales", align_bytes=64)
         regroup(nc.vector.tensor_copy, wfc_grouped[:], wfc_raw[:])
-        total = keep.tile([P, NF], F32, name="total")
-        nc.vector.tensor_copy(out=total[:], in_=a_sb[:])
         nc.vector.quantize_mx(
             out=wfc_codes[:].bitcast(FP8X4), scales=wfc_scales[:], in_=wfc_grouped[:]
         )
@@ -252,20 +271,27 @@ def tile_dtnnstep_pa_kernel(
         def live(n):
             return 0 <= n < ROUNDS
 
-        for s in range(1, ROUNDS + 4):
+        for s in range(1, ROUNDS + 6):
             if live(s):
                 transpose_distances(s)
-            if live(s - 4):
-                add_to_sum(s - 4)
-            if live(s - 1):
-                first_product(s - 1)
-                gate(s - 1)
+            if live(s - 5):
+                add_to_sum(s - 5)
             if live(s):
                 quantise_distances(s)
             if live(s - 2):
-                regroup_gated(s - 2)
                 quantise_gated(s - 2)
             if live(s - 3):
                 second_product(s - 3)
+            if live(s - 1):
+                first_product(s - 1)
+                gate(s - 1)
+                regroup_gated(s - 1)
 
+        sum_T_sb = keep.tile([P, F_CHUNKS, P], F32, name="sum_T_sb")
+        nc.scalar.copy(out=sum_T_sb[:], in_=sum_T[:])
+        total_ps = psum_pair.tile([P, NF], F32, name="total_ps", tag="product")
+        for c in range(F_CHUNKS):
+            nc.tensor.transpose(total_ps[:, c * P : (c + 1) * P], sum_T_sb[:, c, :], ident_f32[:])
+        total = keep.tile([P, NF], F32, name="total")
+        nc.vector.tensor_copy(out=total[:], in_=total_ps[:])
         nc.sync.dma_start(out=out.rearrange("b i f -> (b i) f"), in_=total[:])

@@ -179,9 +179,14 @@ def tile_dtnnstep_pa_kernel(
                     op1=ALU.mult,
                 )
 
-        def regroup_gated(n):
-            g_grouped[n] = ring.tile([P, COLS * PACK], BF16, name="g_grouped", align_bytes=64)
-            regroup(nc.vector.tensor_copy, g_grouped[n][:], planar[n][:])
+        def regroup_gated(n, a):
+            if a == 0:
+                g_grouped[n] = ring.tile([P, COLS * PACK], BF16, name="g_grouped", align_bytes=64)
+            regroup(
+                nc.vector.tensor_copy if a == 0 else nc.scalar.copy,
+                g_grouped[n][:, a * P * PACK : (a + 1) * P * PACK],
+                planar[n][:, :, a * P : (a + 1) * P],
+            )
 
         def quantise_gated(n):
             g_codes[n] = ring.tile([P, COLS], U32, name="g_codes", align_bytes=64)
@@ -279,13 +284,14 @@ def tile_dtnnstep_pa_kernel(
             if live(s):
                 quantise_distances(s)
             if live(s - 2):
+                regroup_gated(s - 2, 1)
                 quantise_gated(s - 2)
             if live(s - 3):
                 second_product(s - 3)
             if live(s - 1):
                 first_product(s - 1)
                 gate(s - 1)
-                regroup_gated(s - 1)
+                regroup_gated(s - 1, 0)
 
         sum_T_sb = keep.tile([P, F_CHUNKS, P], F32, name="sum_T_sb")
         nc.scalar.copy(out=sum_T_sb[:], in_=sum_T[:])

@@ -24,6 +24,7 @@ F_CHUNKS = NF // P
 TILES = 2
 ROUNDS = ATOMS // TILES
 COLS = TILES * P
+LAST_PAIRED = 28
 RUN = 4
 
 FLOPS = 2 * (MOLS * ATOMS * ATOMS * (ND * NH + NH * NF) + MOLS * ATOMS * NF * NH)
@@ -43,7 +44,8 @@ def tile_dtnnstep_pa_kernel(
     with ExitStack() as ctx:
         keep = ctx.enter_context(tc.tile_pool(name="keep", bufs=1))
         ring = ctx.enter_context(tc.tile_pool(name="ring", bufs=3))
-        tanh_pool = ctx.enter_context(tc.tile_pool(name="tanh_pool", bufs=3 * TILES))
+        tanh_pool = ctx.enter_context(tc.tile_pool(name="tanh_pool", bufs=4 * TILES))
+        pair_pool = ctx.enter_context(tc.tile_pool(name="pair_pool", bufs=4))
         psum_flip = ctx.enter_context(tc.psum_pool(name="psum_flip", bufs=2))
         psum_dist = ctx.enter_context(tc.psum_pool(name="psum_dist", bufs=3))
         psum_pair = ctx.enter_context(tc.psum_pool(name="psum_pair", bufs=2))
@@ -115,6 +117,7 @@ def tile_dtnnstep_pa_kernel(
 
         d_grouped, d_codes, d_scales, dist_banks = {}, {}, {}, {}
         planar, g_grouped, g_codes, g_scales, tanh_tiles = {}, {}, {}, {}, {}
+        pair_sums = {}
 
         def transpose_distances(n):
             d_grouped[n] = ring.tile(
@@ -215,17 +218,27 @@ def tile_dtnnstep_pa_kernel(
                 nc.scalar.activation(
                     out=squashed[:], in_=product[:], func=FUNC.Tanh, scale=mask[:, j : j + 1]
                 )
+                if a == 0 and 0 < j <= LAST_PAIRED:
+                    pair_sums[j] = pair_pool.tile([P, NF], F32, name="pair")
+                    nc.gpsimd.tensor_tensor(
+                        out=pair_sums[j][:], in0=tanh_tiles[n - 1][1][:], in1=squashed[:], op=ALU.add
+                    )
 
         def add_to_sum(n):
-            for a in range(TILES):
+            j = n * TILES
+            if j in pair_sums:
+                summands = [pair_sums[j]]
+            else:
+                summands = [tanh_tiles[i // TILES][i % TILES] for i in (j - 1, j) if 0 <= i < ATOMS]
+            for summand in summands:
                 for c in range(F_CHUNKS):
                     nc.tensor.matmul(
                         out=sum_T[:, c, :],
-                        lhsT=tanh_tiles[n][a][:, c * P : (c + 1) * P],
+                        lhsT=summand[:, c * P : (c + 1) * P],
                         rhs=ident_f32[:],
                         is_transpose=True,
                         start=False,
-                        stop=(n == ROUNDS - 1 and a == TILES - 1 and c == F_CHUNKS - 1),
+                        stop=(n == ROUNDS and c == F_CHUNKS - 1),
                     )
 
         aT_ps = psum_pair.tile([P, F_CHUNKS, P], BF16, name="aT_ps", tag="product")
@@ -279,7 +292,7 @@ def tile_dtnnstep_pa_kernel(
         for s in range(1, ROUNDS + 6):
             if live(s):
                 transpose_distances(s)
-            if live(s - 5):
+            if 0 <= s - 5 <= ROUNDS:
                 add_to_sum(s - 5)
             if live(s):
                 quantise_distances(s)

@@ -24,7 +24,7 @@ F_CHUNKS = NF // P
 TILES = 2
 ROUNDS = ATOMS // TILES
 COLS = TILES * P
-LAST_PAIRED = 28
+LAST_PAIRED = 26
 RUN = 4
 
 FLOPS = 2 * (MOLS * ATOMS * ATOMS * (ND * NH + NH * NF) + MOLS * ATOMS * NF * NH)
@@ -182,28 +182,32 @@ def tile_dtnnstep_pa_kernel(
                     op1=ALU.mult,
                 )
 
-        def regroup_gated(n, a):
+        def regroup_gated(n, a, copy):
             if a == 0:
                 g_grouped[n] = ring.tile([P, COLS * PACK], BF16, name="g_grouped", align_bytes=64)
             regroup(
-                nc.vector.tensor_copy if a == 0 else nc.scalar.copy,
+                copy,
                 g_grouped[n][:, a * P * PACK : (a + 1) * P * PACK],
                 planar[n][:, :, a * P : (a + 1) * P],
             )
 
-        def quantise_gated(n):
-            g_codes[n] = ring.tile([P, COLS], U32, name="g_codes", align_bytes=64)
-            g_scales[n] = ring.tile([P, COLS], U8, name="g_scales", align_bytes=64)
+        def quantise_gated(n, first=0, count=TILES):
+            if first == 0:
+                g_codes[n] = ring.tile([P, COLS], U32, name="g_codes", align_bytes=64)
+                g_scales[n] = ring.tile([P, COLS], U8, name="g_scales", align_bytes=64)
+            pairs = slice(first * P, (first + count) * P)
             nc.vector.quantize_mx(
-                out=g_codes[n][:].bitcast(FP8X4), scales=g_scales[n][:], in_=g_grouped[n][:]
+                out=g_codes[n][:, pairs].bitcast(FP8X4),
+                scales=g_scales[n][:, pairs],
+                in_=g_grouped[n][:, pairs.start * PACK : pairs.stop * PACK],
             )
 
-        def second_product(n):
+        def second_product(n, pool=psum_pair, tag="product"):
             tanh_tiles[n] = []
             for a in range(TILES):
                 j = n * TILES + a
                 pairs = slice(a * P, (a + 1) * P)
-                product = psum_pair.tile([P, NF], F32, name="product")
+                product = pool.tile([P, NF], F32, name="product", tag=tag)
                 nc.tensor.matmul_mx(
                     out=product[:],
                     lhsT=g_codes[n][:, pairs].bitcast(FP8X4),
@@ -226,20 +230,16 @@ def tile_dtnnstep_pa_kernel(
 
         def add_to_sum(n):
             j = n * TILES
-            if j in pair_sums:
-                summands = [pair_sums[j]]
-            else:
-                summands = [tanh_tiles[i // TILES][i % TILES] for i in (j - 1, j) if 0 <= i < ATOMS]
-            for summand in summands:
-                for c in range(F_CHUNKS):
-                    nc.tensor.matmul(
-                        out=sum_T[:, c, :],
-                        lhsT=summand[:, c * P : (c + 1) * P],
-                        rhs=ident_f32[:],
-                        is_transpose=True,
-                        start=False,
-                        stop=(n == ROUNDS and c == F_CHUNKS - 1),
-                    )
+            summand = pair_sums[j] if j in pair_sums else tanh_tiles[0][0] if j == 0 else tanh_tiles[n - 1][1]
+            for c in range(F_CHUNKS):
+                nc.tensor.matmul(
+                    out=sum_T[:, c, :],
+                    lhsT=summand[:, c * P : (c + 1) * P],
+                    rhs=ident_f32[:],
+                    is_transpose=True,
+                    start=False,
+                    stop=(j == LAST_PAIRED + TILES and c == F_CHUNKS - 1),
+                )
 
         aT_ps = psum_pair.tile([P, F_CHUNKS, P], BF16, name="aT_ps", tag="product")
         for c in range(F_CHUNKS):
@@ -289,28 +289,52 @@ def tile_dtnnstep_pa_kernel(
         def live(n):
             return 0 <= n < ROUNDS
 
-        for s in range(1, ROUNDS + 6):
-            if live(s):
-                transpose_distances(s)
-            if 0 <= s - 5 <= ROUNDS:
+        for s in range(1, ROUNDS):
+            transpose_distances(s)
+            if live(s - 5):
                 add_to_sum(s - 5)
-            if live(s):
-                quantise_distances(s)
+            quantise_distances(s)
             if live(s - 2):
-                regroup_gated(s - 2, 1)
+                regroup_gated(s - 2, 1, nc.scalar.copy)
                 quantise_gated(s - 2)
             if live(s - 3):
                 second_product(s - 3)
-            if live(s - 1):
-                first_product(s - 1)
-                gate(s - 1)
-                regroup_gated(s - 1, 0)
+            first_product(s - 1)
+            gate(s - 1)
+            regroup_gated(s - 1, 0, nc.vector.tensor_copy)
 
+        last = ROUNDS - 1
+        add_to_sum(last - 4)
+        regroup_gated(last - 1, 1, nc.scalar.copy)
+        quantise_gated(last - 1)
+        second_product(last - 2)
+        first_product(last)
+        second_product(last - 1, psum_flip, "flipped")
+        gate(last)
+        for a in range(TILES):
+            regroup_gated(last, a, nc.vector.tensor_copy)
+        for a in range(TILES):
+            quantise_gated(last, a, 1)
+        for n in range(last - 3, last):
+            add_to_sum(n)
         sum_T_sb = keep.tile([P, F_CHUNKS, P], F32, name="sum_T_sb")
-        nc.scalar.copy(out=sum_T_sb[:], in_=sum_T[:])
-        total_ps = psum_pair.tile([P, NF], F32, name="total_ps", tag="product")
+        nc.vector.tensor_copy(out=sum_T_sb[:], in_=sum_T[:])
+        second_product(last)
+        total_ps = psum_dist.tile([P, NF], F32, name="total_ps", tag="dist_bank")
         for c in range(F_CHUNKS):
             nc.tensor.transpose(total_ps[:, c * P : (c + 1) * P], sum_T_sb[:, c, :], ident_f32[:])
         total = keep.tile([P, NF], F32, name="total")
-        nc.vector.tensor_copy(out=total[:], in_=total_ps[:])
-        nc.sync.dma_start(out=out.rearrange("b i f -> (b i) f"), in_=total[:])
+        halves = [slice(0, NF // 2), slice(NF // 2, NF)]
+        late = [tanh_tiles[n][a] for n in (last - 1, last) for a in range(TILES)]
+        terms = [late[1], late[2], total_ps, late[3]]
+        for k in range(len(terms)):
+            for half in halves:
+                nc.vector.tensor_tensor(
+                    out=total[:, half],
+                    in0=terms[k][:, half],
+                    in1=late[0][:, half] if k == 0 else total[:, half],
+                    op=ALU.add,
+                )
+        out_rows = out.rearrange("b i f -> (b i) f")
+        nc.sync.dma_start(out=out_rows[:, halves[0]], in_=total[:, halves[0]])
+        nc.scalar.dma_start(out=out_rows[:, halves[1]], in_=total[:, halves[1]])

@@ -25,6 +25,7 @@ TILES = 2
 ROUNDS = ATOMS // TILES
 COLS = TILES * P
 LAST_PAIRED = 26
+VECTOR_COLS = 160
 RUN = 4
 
 FLOPS = 2 * (MOLS * ATOMS * ATOMS * (ND * NH + NH * NF) + MOLS * ATOMS * NF * NH)
@@ -182,13 +183,14 @@ def tile_dtnnstep_pa_kernel(
                     op1=ALU.mult,
                 )
 
-        def regroup_gated(n, a, copy):
+        def regroup_gated(n, a, copy, split=VECTOR_COLS):
             if a == 0:
                 g_grouped[n] = ring.tile([P, COLS * PACK], BF16, name="g_grouped", align_bytes=64)
+            pairs = slice(0, split) if a == 0 else slice(split, COLS)
             regroup(
                 copy,
-                g_grouped[n][:, a * P * PACK : (a + 1) * P * PACK],
-                planar[n][:, :, a * P : (a + 1) * P],
+                g_grouped[n][:, pairs.start * PACK : pairs.stop * PACK],
+                planar[n][:, :, pairs],
             )
 
         def quantise_gated(n, first=0, count=TILES):
@@ -312,7 +314,7 @@ def tile_dtnnstep_pa_kernel(
         second_product(last - 1, psum_flip, "flipped")
         gate(last)
         for a in range(TILES):
-            regroup_gated(last, a, nc.vector.tensor_copy)
+            regroup_gated(last, a, nc.vector.tensor_copy, P)
         for a in range(TILES):
             quantise_gated(last, a, 1)
         for n in range(last - 3, last):

@@ -72,16 +72,16 @@ def tile_dtnnstep_pa_kernel(
         wcf_sb = keep.tile([P, F_CHUNKS, NH], BF16, name="wcf_sb")
         nc.sync.dma_start(out=wcf_sb[:], in_=W_cf.rearrange("(c p) h -> p c h", p=P))
         wfc_raw = keep.tile([P, PACK, NF], BF16, name="wfc_raw")
-        nc.sync.dma_start(out=wfc_raw[:], in_=W_fc.rearrange("(p t) f -> p t f", t=PACK))
+        nc.sync.dma_start(out=wfc_raw[:], in_=W_fc.rearrange("(t p) f -> p t f", p=P))
         for n in range(1, ROUNDS):
             load_distances(n)
 
         a_sb = keep.tile([P, NF], BF16, name="a_sb")
         nc.scalar.dma_start(out=a_sb[:], in_=atom_features.rearrange("b n f -> (b n) f"))
         bcf_bf = keep.tile([P, PACK], BF16, name="bcf_bf")
-        nc.scalar.dma_start(out=bcf_bf[:], in_=b_cf.rearrange("(p t) -> p t", t=PACK))
+        nc.scalar.dma_start(out=bcf_bf[:], in_=b_cf.rearrange("(t p) -> p t", p=P))
         bdf_bf = keep.tile([P, PACK], BF16, name="bdf_bf")
-        nc.scalar.dma_start(out=bdf_bf[:], in_=b_df.rearrange("(p t) -> p t", t=PACK))
+        nc.scalar.dma_start(out=bdf_bf[:], in_=b_df.rearrange("(t p) -> p t", p=P))
         mask_bf = keep.tile([P, ATOMS], BF16, name="mask_bf")
         nc.scalar.dma_start(out=mask_bf[:], in_=distance_matrix_mask.rearrange("b i j -> (b i) j"))
 
@@ -95,20 +95,17 @@ def tile_dtnnstep_pa_kernel(
         make_identity(nc, ident_bf[:])
 
         bcf = keep.tile([P, PACK], F32, name="bcf")
-        nc.vector.tensor_copy(out=bcf[:], in_=bcf_bf[:])
+        nc.gpsimd.tensor_copy(out=bcf[:], in_=bcf_bf[:])
         bdf = keep.tile([P, PACK], F32, name="bdf")
-        nc.vector.tensor_copy(out=bdf[:], in_=bdf_bf[:])
+        nc.gpsimd.tensor_copy(out=bdf[:], in_=bdf_bf[:])
         mask = keep.tile([P, ATOMS], F32, name="mask")
-        nc.vector.tensor_copy(out=mask[:], in_=mask_bf[:])
+        nc.gpsimd.tensor_copy(out=mask[:], in_=mask_bf[:])
 
         wdf_grouped = keep.tile([P, D_PASSES, NH * PACK], BF16, name="wdf_grouped", align_bytes=64)
         wdf_codes = keep.tile([P, D_PASSES, NH], U32, name="wdf_codes", align_bytes=64)
         wdf_scales = keep.tile([P, D_PASSES, NH], U8, name="wdf_scales", align_bytes=64)
         for g in range(D_PASSES):
-            nc.vector.tensor_copy(
-                out=wdf_grouped[:, g, :].rearrange("p (t q v) -> p t q v", t=PACK, v=PACK),
-                in_=wdf_raw[:, g, :, :].rearrange("p v (q t) -> p t q v", t=PACK),
-            )
+            regroup(nc.vector.tensor_copy, wdf_grouped[:, g, :], wdf_raw[:, g, :, :])
         for g in range(D_PASSES):
             nc.vector.quantize_mx(
                 out=wdf_codes[:, g, :].bitcast(FP8X4),
@@ -261,12 +258,11 @@ def tile_dtnnstep_pa_kernel(
         quantise_distances(0)
 
         atom_ps = psum_pair.tile([P, PACK, P], F32, name="atom_ps", tag="product")
-        wcf_cols = wcf_sb[:].rearrange("p c (q t) -> p c t q", t=PACK)
         for t in range(PACK):
             for c in range(F_CHUNKS):
                 nc.tensor.matmul(
                     out=atom_ps[:, t, :],
-                    lhsT=wcf_cols[:, c, t, :],
+                    lhsT=wcf_sb[:, c, t * P : (t + 1) * P],
                     rhs=aT[:, c, :],
                     start=(c == 0),
                     stop=(c == F_CHUNKS - 1),

@@ -24,8 +24,9 @@ F_CHUNKS = NF // P
 TILES = 2
 ROUNDS = ATOMS // TILES
 COLS = TILES * P
-LAST_PAIRED = 26
-VECTOR_COLS = 160
+LAST_PAIRED = 24
+FILLING = 5
+VECTOR_COLS = 144, 208
 RUN = 4
 
 FLOPS = 2 * (MOLS * ATOMS * ATOMS * (ND * NH + NH * NF) + MOLS * ATOMS * NF * NH)
@@ -65,15 +66,24 @@ def tile_dtnnstep_pa_kernel(
         d_rows = distance_matrix.rearrange("b i j k -> (b i) j k")
         d_sb = [keep.tile([P, TILES, ND], BF16, name="d%d" % n) for n in range(ROUNDS)]
 
-        def load_distances(n):
-            nc.sync.dma_start(out=d_sb[n][:], in_=d_rows[:, n * TILES : (n + 1) * TILES, :])
+        def load_distances(n, first=0, count=TILES):
+            j = n * TILES + first
+            nc.sync.dma_start(
+                out=d_sb[n][:, first : first + count, :], in_=d_rows[:, j : j + count, :]
+            )
 
-        load_distances(0)
+        for a in range(TILES):
+            load_distances(0, a, 1)
         wcf_sb = keep.tile([P, F_CHUNKS, NH], BF16, name="wcf_sb")
-        nc.sync.dma_start(out=wcf_sb[:], in_=W_cf.rearrange("(c p) h -> p c h", p=P))
+        wcf_rows = W_cf.rearrange("(c p) h -> p c h", p=P)
+        for half in range(2):
+            h_cols = slice(half * (NH // 2), (half + 1) * (NH // 2))
+            nc.sync.dma_start(out=wcf_sb[:, :, h_cols], in_=wcf_rows[:, :, h_cols])
+        for a in range(TILES):
+            load_distances(1, a, 1)
         wfc_raw = keep.tile([P, PACK, NF], BF16, name="wfc_raw")
         nc.sync.dma_start(out=wfc_raw[:], in_=W_fc.rearrange("(t p) f -> p t f", p=P))
-        for n in range(1, ROUNDS):
+        for n in range(2, ROUNDS):
             load_distances(n)
 
         a_sb = keep.tile([P, NF], BF16, name="a_sb")
@@ -147,31 +157,29 @@ def tile_dtnnstep_pa_kernel(
                 out=d_codes[n][:].bitcast(FP8X4), scales=d_scales[n][:], in_=d_grouped[n][:]
             )
 
-        def first_product(n):
-            dist_banks[n] = []
-            for half in range(PACK // 2):
-                bank = psum_dist.tile([P, 2, COLS], F32, name="dist_bank")
-                dist_banks[n].append(bank)
-                for w in range(2):
-                    h_cols = slice((2 * half + w) * P, (2 * half + w + 1) * P)
-                    for g in range(D_PASSES):
-                        pairs = slice(g * COLS, (g + 1) * COLS)
-                        nc.tensor.matmul_mx(
-                            out=bank[:, w, :],
-                            lhsT=wdf_codes[:, g, h_cols].bitcast(FP8X4),
-                            lhsT_scale=wdf_scales[:, g, h_cols],
-                            rhs=d_codes[n][:, pairs].bitcast(FP8X4),
-                            rhs_scale=d_scales[n][:, pairs],
-                            start=(g == 0),
-                            stop=(g == D_PASSES - 1),
-                        )
+        def first_product(n, half):
+            bank = psum_dist.tile([P, 2, COLS], F32, name="dist_bank")
+            dist_banks[n, half] = bank
+            for w in range(2):
+                h_cols = slice((2 * half + w) * P, (2 * half + w + 1) * P)
+                for g in range(D_PASSES):
+                    pairs = slice(g * COLS, (g + 1) * COLS)
+                    nc.tensor.matmul_mx(
+                        out=bank[:, w, :],
+                        lhsT=wdf_codes[:, g, h_cols].bitcast(FP8X4),
+                        lhsT_scale=wdf_scales[:, g, h_cols],
+                        rhs=d_codes[n][:, pairs].bitcast(FP8X4),
+                        rhs_scale=d_scales[n][:, pairs],
+                        start=(g == 0),
+                        stop=(g == D_PASSES - 1),
+                    )
 
         def gate(n):
             planar[n] = ring.tile([P, PACK, COLS], BF16, name="planar")
             for t in range(PACK):
                 nc.vector.scalar_tensor_tensor(
                     out=planar[n][:, t, :].rearrange("p (c i) -> p c i", i=ATOMS),
-                    in0=dist_banks[n][t // 2][:, t % 2, :].rearrange("p (c i) -> p c i", i=ATOMS),
+                    in0=dist_banks[n, t // 2][:, t % 2, :].rearrange("p (c i) -> p c i", i=ATOMS),
                     scalar=bdf[:, t : t + 1],
                     in1=atom_gate[:, t, n * TILES * MOLS : (n + 1) * TILES * MOLS]
                     .unsqueeze(2)
@@ -180,9 +188,11 @@ def tile_dtnnstep_pa_kernel(
                     op1=ALU.mult,
                 )
 
-        def regroup_gated(n, a, copy, split=VECTOR_COLS):
+        def regroup_gated(n, a, copy, split=None):
             if a == 0:
                 g_grouped[n] = ring.tile([P, COLS * PACK], BF16, name="g_grouped", align_bytes=64)
+            if split is None:
+                split = VECTOR_COLS[0] if n < FILLING else VECTOR_COLS[1]
             pairs = slice(0, split) if a == 0 else slice(split, COLS)
             regroup(
                 copy,
@@ -229,16 +239,24 @@ def tile_dtnnstep_pa_kernel(
 
         def add_to_sum(n):
             j = n * TILES
-            summand = pair_sums[j] if j in pair_sums else tanh_tiles[0][0] if j == 0 else tanh_tiles[n - 1][1]
-            for c in range(F_CHUNKS):
-                nc.tensor.matmul(
-                    out=sum_T[:, c, :],
-                    lhsT=summand[:, c * P : (c + 1) * P],
-                    rhs=ident_f32[:],
-                    is_transpose=True,
-                    start=False,
-                    stop=(j == LAST_PAIRED + TILES and c == F_CHUNKS - 1),
-                )
+            last_summed = ATOMS - 2 * TILES - 1
+            if 0 < j <= LAST_PAIRED:
+                summands = [pair_sums[j]]
+            elif j == 0:
+                summands = [tanh_tiles[0][0]]
+            else:
+                summands = [tanh_tiles[i // TILES][i % TILES] for i in range(max(j - 1, LAST_PAIRED + 1), min(j, last_summed) + 1)]
+            for summand in summands:
+                closing = j > last_summed and summand is summands[-1]
+                for c in range(F_CHUNKS):
+                    nc.tensor.matmul(
+                        out=sum_T[:, c, :],
+                        lhsT=summand[:, c * P : (c + 1) * P],
+                        rhs=ident_f32[:],
+                        is_transpose=True,
+                        start=False,
+                        stop=(closing and c == F_CHUNKS - 1),
+                    )
 
         aT_ps = psum_pair.tile([P, F_CHUNKS, P], BF16, name="aT_ps", tag="product")
         for c in range(F_CHUNKS):
@@ -257,61 +275,68 @@ def tile_dtnnstep_pa_kernel(
         transpose_distances(0)
         quantise_distances(0)
 
-        atom_ps = psum_pair.tile([P, PACK, P], F32, name="atom_ps", tag="product")
-        for t in range(PACK):
-            for c in range(F_CHUNKS):
-                nc.tensor.matmul(
-                    out=atom_ps[:, t, :],
-                    lhsT=wcf_sb[:, c, t * P : (t + 1) * P],
-                    rhs=aT[:, c, :],
-                    start=(c == 0),
-                    stop=(c == F_CHUNKS - 1),
-                )
         atom_gate = keep.tile([P, PACK, ATOMS * MOLS], F32, name="atom_gate")
-        for t in range(PACK):
-            nc.scalar.activation(
-                out=atom_gate[:, t, :].rearrange("p (j b) -> p j b", b=MOLS),
-                in_=atom_ps[:, t, :].rearrange("p (b j) -> p j b", b=MOLS),
-                func=FUNC.Identity,
-                bias=bcf[:, t : t + 1],
-            )
+        for half in range(2):
+            atom_ps = psum_pair.tile([P, 2, P], F32, name="atom_ps", tag="product")
+            for w in range(2):
+                t = 2 * half + w
+                for c in range(F_CHUNKS):
+                    nc.tensor.matmul(
+                        out=atom_ps[:, w, :],
+                        lhsT=wcf_sb[:, c, t * P : (t + 1) * P],
+                        rhs=aT[:, c, :],
+                        start=(c == 0),
+                        stop=(c == F_CHUNKS - 1),
+                    )
+            for w in range(2):
+                t = 2 * half + w
+                nc.scalar.activation(
+                    out=atom_gate[:, t, :].rearrange("p (j b) -> p j b", b=MOLS),
+                    in_=atom_ps[:, w, :].rearrange("p (b j) -> p j b", b=MOLS),
+                    func=FUNC.Identity,
+                    bias=bcf[:, t : t + 1],
+                )
 
         wfc_grouped = keep.tile([P, NF * PACK], BF16, name="wfc_grouped", align_bytes=64)
         wfc_codes = keep.tile([P, NF], U32, name="wfc_codes", align_bytes=64)
         wfc_scales = keep.tile([P, NF], U8, name="wfc_scales", align_bytes=64)
-        regroup(nc.vector.tensor_copy, wfc_grouped[:], wfc_raw[:])
-        nc.vector.quantize_mx(
-            out=wfc_codes[:].bitcast(FP8X4), scales=wfc_scales[:], in_=wfc_grouped[:]
-        )
+        half_cols = NF // 2
 
-        def live(n):
-            return 0 <= n < ROUNDS
+        transpose_distances(1)
+        regroup(nc.vector.tensor_copy, wfc_grouped[:, : half_cols * PACK], wfc_raw[:, :, :half_cols])
+        regroup(nc.scalar.copy, wfc_grouped[:, half_cols * PACK :], wfc_raw[:, :, half_cols:])
 
-        for s in range(1, ROUNDS):
-            transpose_distances(s)
-            if live(s - 5):
-                add_to_sum(s - 5)
-            quantise_distances(s)
-            if live(s - 2):
-                regroup_gated(s - 2, 1, nc.scalar.copy)
-                quantise_gated(s - 2)
-            if live(s - 3):
-                second_product(s - 3)
-            first_product(s - 1)
-            gate(s - 1)
-            regroup_gated(s - 1, 0, nc.vector.tensor_copy)
+        for s in range(ROUNDS - 1):
+            if s > 0:
+                transpose_distances(s + 1)
+            if s >= 4:
+                add_to_sum(s - 4)
+            quantise_distances(s + 1)
+            if s >= 1:
+                regroup_gated(s - 1, 1, nc.scalar.copy)
+                quantise_gated(s - 1)
+            first_product(s, 0)
+            if s >= 2:
+                second_product(s - 2)
+            first_product(s, 1)
+            gate(s)
+            regroup_gated(s, 0, nc.vector.tensor_copy)
+            if s == 0:
+                nc.vector.quantize_mx(
+                    out=wfc_codes[:].bitcast(FP8X4), scales=wfc_scales[:], in_=wfc_grouped[:]
+                )
 
         last = ROUNDS - 1
         add_to_sum(last - 4)
         regroup_gated(last - 1, 1, nc.scalar.copy)
         quantise_gated(last - 1)
+        first_product(last, 0)
         second_product(last - 2)
-        first_product(last)
+        first_product(last, 1)
         second_product(last - 1, psum_flip, "flipped")
         gate(last)
         for a in range(TILES):
             regroup_gated(last, a, nc.vector.tensor_copy, P)
-        for a in range(TILES):
             quantise_gated(last, a, 1)
         for n in range(last - 3, last):
             add_to_sum(n)

@@ -25,8 +25,7 @@ TILES = 2
 ROUNDS = ATOMS // TILES
 COLS = TILES * P
 LAST_PAIRED = 24
-FILLING = 5
-VECTOR_COLS = 144, 208
+VECTOR_COLS = 160
 RUN = 4
 
 FLOPS = 2 * (MOLS * ATOMS * ATOMS * (ND * NH + NH * NF) + MOLS * ATOMS * NF * NH)
@@ -188,11 +187,9 @@ def tile_dtnnstep_pa_kernel(
                     op1=ALU.mult,
                 )
 
-        def regroup_gated(n, a, copy, split=None):
+        def regroup_gated(n, a, copy, split=VECTOR_COLS):
             if a == 0:
                 g_grouped[n] = ring.tile([P, COLS * PACK], BF16, name="g_grouped", align_bytes=64)
-            if split is None:
-                split = VECTOR_COLS[0] if n < FILLING else VECTOR_COLS[1]
             pairs = slice(0, split) if a == 0 else slice(split, COLS)
             regroup(
                 copy,
@@ -300,11 +297,9 @@ def tile_dtnnstep_pa_kernel(
         wfc_grouped = keep.tile([P, NF * PACK], BF16, name="wfc_grouped", align_bytes=64)
         wfc_codes = keep.tile([P, NF], U32, name="wfc_codes", align_bytes=64)
         wfc_scales = keep.tile([P, NF], U8, name="wfc_scales", align_bytes=64)
-        half_cols = NF // 2
 
         transpose_distances(1)
-        regroup(nc.vector.tensor_copy, wfc_grouped[:, : half_cols * PACK], wfc_raw[:, :, :half_cols])
-        regroup(nc.scalar.copy, wfc_grouped[:, half_cols * PACK :], wfc_raw[:, :, half_cols:])
+        regroup(nc.scalar.copy, wfc_grouped[:], wfc_raw[:])
 
         for s in range(ROUNDS - 1):
             if s > 0:
@@ -341,7 +336,7 @@ def tile_dtnnstep_pa_kernel(
         for n in range(last - 3, last):
             add_to_sum(n)
         sum_T_sb = keep.tile([P, F_CHUNKS, P], F32, name="sum_T_sb")
-        nc.vector.tensor_copy(out=sum_T_sb[:], in_=sum_T[:])
+        nc.scalar.copy(out=sum_T_sb[:], in_=sum_T[:])
         second_product(last)
         total_ps = psum_dist.tile([P, NF], F32, name="total_ps", tag="dist_bank")
         for c in range(F_CHUNKS):

@@ -65,21 +65,13 @@ def tile_dtnnstep_pa_kernel(
         d_rows = distance_matrix.rearrange("b i j k -> (b i) j k")
         d_sb = [keep.tile([P, TILES, ND], BF16, name="d%d" % n) for n in range(ROUNDS)]
 
-        def load_distances(n, first=0, count=TILES):
-            j = n * TILES + first
-            nc.sync.dma_start(
-                out=d_sb[n][:, first : first + count, :], in_=d_rows[:, j : j + count, :]
-            )
+        def load_distances(n):
+            nc.sync.dma_start(out=d_sb[n][:], in_=d_rows[:, n * TILES : (n + 1) * TILES, :])
 
-        for a in range(TILES):
-            load_distances(0, a, 1)
+        load_distances(0)
         wcf_sb = keep.tile([P, F_CHUNKS, NH], BF16, name="wcf_sb")
-        wcf_rows = W_cf.rearrange("(c p) h -> p c h", p=P)
-        for half in range(2):
-            h_cols = slice(half * (NH // 2), (half + 1) * (NH // 2))
-            nc.sync.dma_start(out=wcf_sb[:, :, h_cols], in_=wcf_rows[:, :, h_cols])
-        for a in range(TILES):
-            load_distances(1, a, 1)
+        nc.sync.dma_start(out=wcf_sb[:], in_=W_cf.rearrange("(p c) h -> p c h", c=F_CHUNKS))
+        load_distances(1)
         wfc_raw = keep.tile([P, PACK, NF], BF16, name="wfc_raw")
         nc.sync.dma_start(out=wfc_raw[:], in_=W_fc.rearrange("(t p) f -> p t f", p=P))
         for n in range(2, ROUNDS):
@@ -87,10 +79,12 @@ def tile_dtnnstep_pa_kernel(
 
         a_sb = keep.tile([P, NF], BF16, name="a_sb")
         nc.scalar.dma_start(out=a_sb[:], in_=atom_features.rearrange("b n f -> (b n) f"))
-        bcf_bf = keep.tile([P, PACK], BF16, name="bcf_bf")
-        nc.scalar.dma_start(out=bcf_bf[:], in_=b_cf.rearrange("(t p) -> p t", p=P))
-        bdf_bf = keep.tile([P, PACK], BF16, name="bdf_bf")
-        nc.scalar.dma_start(out=bdf_bf[:], in_=b_df.rearrange("(t p) -> p t", p=P))
+        bias_rows = keep.tile([P, P], BF16, name="bias_rows")
+        nc.vector.memset(bias_rows[:], 0.0)
+        for i, b in enumerate((b_cf, b_df)):
+            nc.scalar.dma_start(
+                out=bias_rows[i * PACK : (i + 1) * PACK, :], in_=b.rearrange("(t p) -> t p", p=P)
+            )
         mask_bf = keep.tile([P, ATOMS], BF16, name="mask_bf")
         nc.scalar.dma_start(out=mask_bf[:], in_=distance_matrix_mask.rearrange("b i j -> (b i) j"))
 
@@ -103,10 +97,6 @@ def tile_dtnnstep_pa_kernel(
         ident_bf = keep.tile([P, P], BF16, name="ident_bf")
         make_identity(nc, ident_bf[:])
 
-        bcf = keep.tile([P, PACK], F32, name="bcf")
-        nc.gpsimd.tensor_copy(out=bcf[:], in_=bcf_bf[:])
-        bdf = keep.tile([P, PACK], F32, name="bdf")
-        nc.gpsimd.tensor_copy(out=bdf[:], in_=bdf_bf[:])
         mask = keep.tile([P, ATOMS], F32, name="mask")
         nc.gpsimd.tensor_copy(out=mask[:], in_=mask_bf[:])
 
@@ -255,11 +245,21 @@ def tile_dtnnstep_pa_kernel(
                         stop=(closing and c == F_CHUNKS - 1),
                     )
 
-        aT_ps = psum_pair.tile([P, F_CHUNKS, P], BF16, name="aT_ps", tag="product")
-        for c in range(F_CHUNKS):
-            nc.tensor.transpose(aT_ps[:, c, :], a_sb[:, c * P : (c + 1) * P], ident_bf[:])
         aT = keep.tile([P, F_CHUNKS, P], BF16, name="aT")
-        nc.scalar.copy(out=aT[:], in_=aT_ps[:])
+        aT_cf = keep.tile([P, F_CHUNKS, P], BF16, name="aT_cf")
+        for turned, chunks in (
+            (aT_cf, a_sb[:].rearrange("m (q c) -> m c q", c=F_CHUNKS)),
+            (aT, a_sb[:].rearrange("m (c q) -> m c q", c=F_CHUNKS)),
+        ):
+            aT_ps = psum_pair.tile([P, F_CHUNKS, P], BF16, name="aT_ps", tag="product")
+            for c in range(F_CHUNKS):
+                nc.tensor.transpose(aT_ps[:, c, :], chunks[:, c, :], ident_bf[:])
+            nc.scalar.copy(out=turned[:], in_=aT_ps[:])
+        bias_ps = psum_flip.tile([P, P], BF16, name="bias_ps", tag="flipped")
+        nc.tensor.transpose(bias_ps[:], bias_rows[:], ident_bf[:])
+        biases = keep.tile([P, 2 * PACK], F32, name="biases")
+        nc.scalar.copy(out=biases[:], in_=bias_ps[:, : 2 * PACK])
+        bcf, bdf = biases[:, :PACK], biases[:, PACK:]
         sum_T = psum_sum.tile([P, F_CHUNKS, P], F32, name="sum_T")
         nc.tensor.matmul(
             out=sum_T[:].rearrange("q c m -> q (c m)"),
@@ -281,7 +281,7 @@ def tile_dtnnstep_pa_kernel(
                     nc.tensor.matmul(
                         out=atom_ps[:, w, :],
                         lhsT=wcf_sb[:, c, t * P : (t + 1) * P],
-                        rhs=aT[:, c, :],
+                        rhs=aT_cf[:, c, :],
                         start=(c == 0),
                         stop=(c == F_CHUNKS - 1),
                     )
@@ -299,7 +299,9 @@ def tile_dtnnstep_pa_kernel(
         wfc_scales = keep.tile([P, NF], U8, name="wfc_scales", align_bytes=64)
 
         transpose_distances(1)
-        regroup(nc.scalar.copy, wfc_grouped[:], wfc_raw[:])
+        half_cols = NF // 2
+        regroup(nc.scalar.copy, wfc_grouped[:, : half_cols * PACK], wfc_raw[:, :, :half_cols])
+        regroup(nc.vector.tensor_copy, wfc_grouped[:, half_cols * PACK :], wfc_raw[:, :, half_cols:])
 
         for s in range(ROUNDS - 1):
             if s > 0:
@@ -315,11 +317,11 @@ def tile_dtnnstep_pa_kernel(
                 second_product(s - 2)
             first_product(s, 1)
             gate(s)
-            regroup_gated(s, 0, nc.vector.tensor_copy)
             if s == 0:
                 nc.vector.quantize_mx(
                     out=wfc_codes[:].bitcast(FP8X4), scales=wfc_scales[:], in_=wfc_grouped[:]
                 )
+            regroup_gated(s, 0, nc.vector.tensor_copy)
 
         last = ROUNDS - 1
         add_to_sum(last - 4)
@@ -332,11 +334,12 @@ def tile_dtnnstep_pa_kernel(
         gate(last)
         for a in range(TILES):
             regroup_gated(last, a, nc.vector.tensor_copy, P)
+        for a in range(TILES):
             quantise_gated(last, a, 1)
         for n in range(last - 3, last):
             add_to_sum(n)
         sum_T_sb = keep.tile([P, F_CHUNKS, P], F32, name="sum_T_sb")
-        nc.scalar.copy(out=sum_T_sb[:], in_=sum_T[:])
+        nc.vector.tensor_copy(out=sum_T_sb[:], in_=sum_T[:])
         second_product(last)
         total_ps = psum_dist.tile([P, NF], F32, name="total_ps", tag="dist_bank")
         for c in range(F_CHUNKS):

@@ -25,6 +25,8 @@ TILES = 2
 ROUNDS = ATOMS // TILES
 COLS = TILES * P
 LAST_PAIRED = 24
+ADD_LAG = 5
+JOINED = 7
 VECTOR_COLS = 160
 RUN = 4
 
@@ -46,7 +48,7 @@ def tile_dtnnstep_pa_kernel(
         keep = ctx.enter_context(tc.tile_pool(name="keep", bufs=1))
         ring = ctx.enter_context(tc.tile_pool(name="ring", bufs=3))
         tanh_pool = ctx.enter_context(tc.tile_pool(name="tanh_pool", bufs=4 * TILES))
-        pair_pool = ctx.enter_context(tc.tile_pool(name="pair_pool", bufs=4))
+        pair_pool = ctx.enter_context(tc.tile_pool(name="pair_pool", bufs=8))
         psum_flip = ctx.enter_context(tc.psum_pool(name="psum_flip", bufs=2))
         psum_dist = ctx.enter_context(tc.psum_pool(name="psum_dist", bufs=3))
         psum_pair = ctx.enter_context(tc.psum_pool(name="psum_pair", bufs=2))
@@ -306,12 +308,17 @@ def tile_dtnnstep_pa_kernel(
         for s in range(ROUNDS - 1):
             if s > 0:
                 transpose_distances(s + 1)
-            if s >= 4:
-                add_to_sum(s - 4)
+            if s >= ADD_LAG and s - ADD_LAG != JOINED - 1:
+                add_to_sum(s - ADD_LAG)
             quantise_distances(s + 1)
             if s >= 1:
                 regroup_gated(s - 1, 1, nc.scalar.copy)
                 quantise_gated(s - 1)
+            if s == JOINED + 3:
+                j = JOINED * TILES
+                nc.vector.tensor_tensor(
+                    out=pair_sums[j][:], in0=pair_sums[j - TILES][:], in1=pair_sums[j][:], op=ALU.add
+                )
             first_product(s, 0)
             if s >= 2:
                 second_product(s - 2)
@@ -324,7 +331,8 @@ def tile_dtnnstep_pa_kernel(
             regroup_gated(s, 0, nc.vector.tensor_copy)
 
         last = ROUNDS - 1
-        add_to_sum(last - 4)
+        for n in range(last - ADD_LAG, last - 3):
+            add_to_sum(n)
         regroup_gated(last - 1, 1, nc.scalar.copy)
         quantise_gated(last - 1)
         first_product(last, 0)

@@ -26,7 +26,6 @@ ROUNDS = ATOMS // TILES
 COLS = TILES * P
 LAST_PAIRED = 24
 ADD_LAG = 5
-JOINED = 7
 VECTOR_COLS = 160
 RUN = 4
 
@@ -48,7 +47,7 @@ def tile_dtnnstep_pa_kernel(
         keep = ctx.enter_context(tc.tile_pool(name="keep", bufs=1))
         ring = ctx.enter_context(tc.tile_pool(name="ring", bufs=3))
         tanh_pool = ctx.enter_context(tc.tile_pool(name="tanh_pool", bufs=4 * TILES))
-        pair_pool = ctx.enter_context(tc.tile_pool(name="pair_pool", bufs=8))
+        pair_pool = ctx.enter_context(tc.tile_pool(name="pair_pool", bufs=5))
         psum_flip = ctx.enter_context(tc.psum_pool(name="psum_flip", bufs=2))
         psum_dist = ctx.enter_context(tc.psum_pool(name="psum_dist", bufs=3))
         psum_pair = ctx.enter_context(tc.psum_pool(name="psum_pair", bufs=2))
@@ -308,17 +307,12 @@ def tile_dtnnstep_pa_kernel(
         for s in range(ROUNDS - 1):
             if s > 0:
                 transpose_distances(s + 1)
-            if s >= ADD_LAG and s - ADD_LAG != JOINED - 1:
+            if s >= ADD_LAG:
                 add_to_sum(s - ADD_LAG)
             quantise_distances(s + 1)
             if s >= 1:
                 regroup_gated(s - 1, 1, nc.scalar.copy)
                 quantise_gated(s - 1)
-            if s == JOINED + 3:
-                j = JOINED * TILES
-                nc.vector.tensor_tensor(
-                    out=pair_sums[j][:], in0=pair_sums[j - TILES][:], in1=pair_sums[j][:], op=ALU.add
-                )
             first_product(s, 0)
             if s >= 2:
                 second_product(s - 2)

from contextlib import ExitStack

import concourse.mybir as mybir
from concourse.masks import make_identity

F32 = mybir.dt.float32
BF16 = mybir.dt.bfloat16
U32 = mybir.dt.uint32
U8 = mybir.dt.uint8
FP8X4 = mybir.dt.float8_e4m3fn_x4
FUNC = mybir.ActivationFunctionType
ALU = mybir.AluOpType

P = 128
PACK = 4
K_PASS = P * PACK

MOLS, ATOMS = 4, 32
NF, ND, NH = 512, 1024, 512
assert MOLS * ATOMS == P and NH == K_PASS

D_PASSES = ND // K_PASS
F_CHUNKS = NF // P
TILES = 2
ROUNDS = ATOMS // TILES
COLS = TILES * P
LAST_PAIRED = 24
ADD_LAG = 5
VECTOR_COLS = 160
RUN = 4

FLOPS = 2 * (MOLS * ATOMS * ATOMS * (ND * NH + NH * NF) + MOLS * ATOMS * NF * NH)


def regroup(copy, grouped, rows):
    copy(
        out=grouped.rearrange("p (c i t) -> p c t i", i=RUN, t=PACK),
        in_=rows.rearrange("p t (c i) -> p c t i", i=RUN),
    )


def tile_dtnnstep_pa_kernel(
    tc, atom_features, distance_matrix, distance_matrix_mask, W_cf, W_df, W_fc, b_cf, b_df, out
):
    nc = tc.nc
    with ExitStack() as ctx:
        keep = ctx.enter_context(tc.tile_pool(name="keep", bufs=1))
        ring = ctx.enter_context(tc.tile_pool(name="ring", bufs=3))
        tanh_pool = ctx.enter_context(tc.tile_pool(name="tanh_pool", bufs=4 * TILES))
        pair_pool = ctx.enter_context(tc.tile_pool(name="pair_pool", bufs=5))
        psum_flip = ctx.enter_context(tc.psum_pool(name="psum_flip", bufs=2))
        psum_dist = ctx.enter_context(tc.psum_pool(name="psum_dist", bufs=3))
        psum_pair = ctx.enter_context(tc.psum_pool(name="psum_pair", bufs=2))
        psum_sum = ctx.enter_context(tc.psum_pool(name="psum_sum", bufs=1))
        ctx.enter_context(tc.manual_schedule())

        wdf_raw = keep.tile([P, D_PASSES, PACK, NH], BF16, name="wdf_raw")
        for g in range(D_PASSES):
            nc.sync.dma_start(
                out=wdf_raw[:, g, :, :].rearrange("q (u e) h -> q u (e h)", e=2),
                in_=W_df[g * K_PASS : (g + 1) * K_PASS, :].rearrange(
                    "(u q e) h -> q u (e h)", q=P, e=2
                ),
            )

        d_rows = distance_matrix.rearrange("b i j k -> (b i) j k")
        d_sb = [keep.tile([P, TILES, ND], BF16, name="d%d" % n) for n in range(ROUNDS)]

        def load_distances(n):
            nc.sync.dma_start(out=d_sb[n][:], in_=d_rows[:, n * TILES : (n + 1) * TILES, :])

        load_distances(0)
        wcf_sb = keep.tile([P, F_CHUNKS, NH], BF16, name="wcf_sb")
        nc.sync.dma_start(out=wcf_sb[:], in_=W_cf.rearrange("(p c) h -> p c h", c=F_CHUNKS))
        load_distances(1)
        wfc_raw = keep.tile([P, PACK, NF], BF16, name="wfc_raw")
        nc.sync.dma_start(out=wfc_raw[:], in_=W_fc.rearrange("(t p) f -> p t f", p=P))
        for n in range(2, ROUNDS):
            load_distances(n)

        a_sb = keep.tile([P, NF], BF16, name="a_sb")
        nc.scalar.dma_start(out=a_sb[:], in_=atom_features.rearrange("b n f -> (b n) f"))
        bias_rows = keep.tile([P, P], BF16, name="bias_rows")
        nc.vector.memset(bias_rows[:], 0.0)
        for i, b in enumerate((b_cf, b_df)):
            nc.scalar.dma_start(
                out=bias_rows[i * PACK : (i + 1) * PACK, :], in_=b.rearrange("(t p) -> t p", p=P)
            )
        mask_bf = keep.tile([P, ATOMS], BF16, name="mask_bf")
        nc.scalar.dma_start(out=mask_bf[:], in_=distance_matrix_mask.rearrange("b i j -> (b i) j"))

        warm = keep.tile([P, 1], F32, name="warm")
        nc.vector.memset(warm[:], 0.0)
        nc.scalar.activation(out=warm[:], in_=warm[:], func=FUNC.Tanh)

        ident_f32 = keep.tile([P, P], F32, name="ident_f32")
        make_identity(nc, ident_f32[:])
        ident_bf = keep.tile([P, P], BF16, name="ident_bf")
        make_identity(nc, ident_bf[:])

        mask = keep.tile([P, ATOMS], F32, name="mask")
        nc.gpsimd.tensor_copy(out=mask[:], in_=mask_bf[:])

        wdf_grouped = keep.tile([P, D_PASSES, NH * PACK], BF16, name="wdf_grouped", align_bytes=64)
        wdf_codes = keep.tile([P, D_PASSES, NH], U32, name="wdf_codes", align_bytes=64)
        wdf_scales = keep.tile([P, D_PASSES, NH], U8, name="wdf_scales", align_bytes=64)
        for g in range(D_PASSES):
            regroup(nc.vector.tensor_copy, wdf_grouped[:, g, :], wdf_raw[:, g, :, :])
        for g in range(D_PASSES):
            nc.vector.quantize_mx(
                out=wdf_codes[:, g, :].bitcast(FP8X4),
                scales=wdf_scales[:, g, :],
                in_=wdf_grouped[:, g, :],
            )

        d_grouped, d_codes, d_scales, dist_banks = {}, {}, {}, {}
        planar, g_grouped, g_codes, g_scales, tanh_tiles = {}, {}, {}, {}, {}
        pair_sums = {}

        def transpose_distances(n):
            d_grouped[n] = ring.tile(
                [P, D_PASSES * COLS * PACK], BF16, name="d_grouped", align_bytes=64
            )
            grouped_words = (
                d_grouped[n][:]
                .bitcast(F32)
                .rearrange("p (g a m u) -> p a g m u", g=D_PASSES, a=TILES, u=2)
            )
            for a in range(TILES):
                words = d_sb[n][:, a, :].bitcast(F32)
                flipped = psum_flip.tile([P, D_PASSES, 2, P], F32, name="flipped")
                for g in range(D_PASSES):
                    for u in range(2):
                        first = (2 * g + u) * P
                        nc.tensor.transpose(
                            flipped[:, g, u, :], words[:, first : first + P], ident_f32[:]
                        )
                nc.scalar.copy(
                    out=grouped_words[:, a, :, :, :],
                    in_=flipped[:].rearrange("p g u m -> p g m u"),
                )

        def quantise_distances(n):
            d_codes[n] = ring.tile([P, D_PASSES * COLS], U32, name="d_codes", align_bytes=64)
            d_scales[n] = ring.tile([P, D_PASSES * COLS], U8, name="d_scales", align_bytes=64)
            nc.vector.quantize_mx(
                out=d_codes[n][:].bitcast(FP8X4), scales=d_scales[n][:], in_=d_grouped[n][:]
            )

        def first_product(n, half):
            bank = psum_dist.tile([P, 2, COLS], F32, name="dist_bank")
            dist_banks[n, half] = bank
            for w in range(2):
                h_cols = slice((2 * half + w) * P, (2 * half + w + 1) * P)
                for g in range(D_PASSES):
                    pairs = slice(g * COLS, (g + 1) * COLS)
                    nc.tensor.matmul_mx(
                        out=bank[:, w, :],
                        lhsT=wdf_codes[:, g, h_cols].bitcast(FP8X4),
                        lhsT_scale=wdf_scales[:, g, h_cols],
                        rhs=d_codes[n][:, pairs].bitcast(FP8X4),
                        rhs_scale=d_scales[n][:, pairs],
                        start=(g == 0),
                        stop=(g == D_PASSES - 1),
                    )

        def gate(n):
            planar[n] = ring.tile([P, PACK, COLS], BF16, name="planar")
            for t in range(PACK):
                nc.vector.scalar_tensor_tensor(
                    out=planar[n][:, t, :].rearrange("p (c i) -> p c i", i=ATOMS),
                    in0=dist_banks[n, t // 2][:, t % 2, :].rearrange("p (c i) -> p c i", i=ATOMS),
                    scalar=bdf[:, t : t + 1],
                    in1=atom_gate[:, t, n * TILES * MOLS : (n + 1) * TILES * MOLS]
                    .unsqueeze(2)
                    .to_broadcast([P, TILES * MOLS, ATOMS]),
                    op0=ALU.add,
                    op1=ALU.mult,
                )

        def regroup_gated(n, a, copy, split=VECTOR_COLS):
            if a == 0:
                g_grouped[n] = ring.tile([P, COLS * PACK], BF16, name="g_grouped", align_bytes=64)
            pairs = slice(0, split) if a == 0 else slice(split, COLS)
            regroup(
                copy,
                g_grouped[n][:, pairs.start * PACK : pairs.stop * PACK],
                planar[n][:, :, pairs],
            )

        def quantise_gated(n, first=0, count=TILES):
            if first == 0:
                g_codes[n] = ring.tile([P, COLS], U32, name="g_codes", align_bytes=64)
                g_scales[n] = ring.tile([P, COLS], U8, name="g_scales", align_bytes=64)
            pairs = slice(first * P, (first + count) * P)
            nc.vector.quantize_mx(
                out=g_codes[n][:, pairs].bitcast(FP8X4),
                scales=g_scales[n][:, pairs],
                in_=g_grouped[n][:, pairs.start * PACK : pairs.stop * PACK],
            )

        def second_product(n, pool=psum_pair, tag="product"):
            tanh_tiles[n] = []
            for a in range(TILES):
                j = n * TILES + a
                pairs = slice(a * P, (a + 1) * P)
                product = pool.tile([P, NF], F32, name="product", tag=tag)
                nc.tensor.matmul_mx(
                    out=product[:],
                    lhsT=g_codes[n][:, pairs].bitcast(FP8X4),
                    lhsT_scale=g_scales[n][:, pairs],
                    rhs=wfc_codes[:].bitcast(FP8X4),
                    rhs_scale=wfc_scales[:],
                    start=True,
                    stop=True,
                )
                squashed = tanh_pool.tile([P, NF], F32, name="squashed")
                tanh_tiles[n].append(squashed)
                nc.scalar.activation(
                    out=squashed[:], in_=product[:], func=FUNC.Tanh, scale=mask[:, j : j + 1]
                )
                if a == 0 and 0 < j <= LAST_PAIRED:
                    pair_sums[j] = pair_pool.tile([P, NF], F32, name="pair")
                    nc.gpsimd.tensor_tensor(
                        out=pair_sums[j][:], in0=tanh_tiles[n - 1][1][:], in1=squashed[:], op=ALU.add
                    )

        def add_to_sum(n):
            j = n * TILES
            last_summed = ATOMS - 2 * TILES - 1
            if 0 < j <= LAST_PAIRED:
                summands = [pair_sums[j]]
            elif j == 0:
                summands = [tanh_tiles[0][0]]
            else:
                summands = [tanh_tiles[i // TILES][i % TILES] for i in range(max(j - 1, LAST_PAIRED + 1), min(j, last_summed) + 1)]
            for summand in summands:
                closing = j > last_summed and summand is summands[-1]
                for c in range(F_CHUNKS):
                    nc.tensor.matmul(
                        out=sum_T[:, c, :],
                        lhsT=summand[:, c * P : (c + 1) * P],
                        rhs=ident_f32[:],
                        is_transpose=True,
                        start=False,
                        stop=(closing and c == F_CHUNKS - 1),
                    )

        aT = keep.tile([P, F_CHUNKS, P], BF16, name="aT")
        aT_cf = keep.tile([P, F_CHUNKS, P], BF16, name="aT_cf")
        for turned, chunks in (
            (aT_cf, a_sb[:].rearrange("m (q c) -> m c q", c=F_CHUNKS)),
            (aT, a_sb[:].rearrange("m (c q) -> m c q", c=F_CHUNKS)),
        ):
            aT_ps = psum_pair.tile([P, F_CHUNKS, P], BF16, name="aT_ps", tag="product")
            for c in range(F_CHUNKS):
                nc.tensor.transpose(aT_ps[:, c, :], chunks[:, c, :], ident_bf[:])
            nc.scalar.copy(out=turned[:], in_=aT_ps[:])
        bias_ps = psum_flip.tile([P, P], BF16, name="bias_ps", tag="flipped")
        nc.tensor.transpose(bias_ps[:], bias_rows[:], ident_bf[:])
        biases = keep.tile([P, 2 * PACK], F32, name="biases")
        nc.scalar.copy(out=biases[:], in_=bias_ps[:, : 2 * PACK])
        bcf, bdf = biases[:, :PACK], biases[:, PACK:]
        sum_T = psum_sum.tile([P, F_CHUNKS, P], F32, name="sum_T")
        nc.tensor.matmul(
            out=sum_T[:].rearrange("q c m -> q (c m)"),
            lhsT=ident_bf[:],
            rhs=aT[:].rearrange("q c m -> q (c m)"),
            start=True,
            stop=False,
        )

        transpose_distances(0)
        quantise_distances(0)

        atom_gate = keep.tile([P, PACK, ATOMS * MOLS], F32, name="atom_gate")
        for half in range(2):
            atom_ps = psum_pair.tile([P, 2, P], F32, name="atom_ps", tag="product")
            for w in range(2):
                t = 2 * half + w
                for c in range(F_CHUNKS):
                    nc.tensor.matmul(
                        out=atom_ps[:, w, :],
                        lhsT=wcf_sb[:, c, t * P : (t + 1) * P],
                        rhs=aT_cf[:, c, :],
                        start=(c == 0),
                        stop=(c == F_CHUNKS - 1),
                    )
            for w in range(2):
                t = 2 * half + w
                nc.scalar.activation(
                    out=atom_gate[:, t, :].rearrange("p (j b) -> p j b", b=MOLS),
                    in_=atom_ps[:, w, :].rearrange("p (b j) -> p j b", b=MOLS),
                    func=FUNC.Identity,
                    bias=bcf[:, t : t + 1],
                )

        wfc_grouped = keep.tile([P, NF * PACK], BF16, name="wfc_grouped", align_bytes=64)
        wfc_codes = keep.tile([P, NF], U32, name="wfc_codes", align_bytes=64)
        wfc_scales = keep.tile([P, NF], U8, name="wfc_scales", align_bytes=64)

        transpose_distances(1)
        half_cols = NF // 2
        regroup(nc.scalar.copy, wfc_grouped[:, : half_cols * PACK], wfc_raw[:, :, :half_cols])
        regroup(nc.vector.tensor_copy, wfc_grouped[:, half_cols * PACK :], wfc_raw[:, :, half_cols:])

        for s in range(ROUNDS - 1):
            if s > 0:
                transpose_distances(s + 1)
            if s >= ADD_LAG:
                add_to_sum(s - ADD_LAG)
            quantise_distances(s + 1)
            if s >= 1:
                regroup_gated(s - 1, 1, nc.scalar.copy)
                quantise_gated(s - 1)
            first_product(s, 0)
            if s >= 2:
                second_product(s - 2)
            first_product(s, 1)
            gate(s)
            if s == 0:
                nc.vector.quantize_mx(
                    out=wfc_codes[:].bitcast(FP8X4), scales=wfc_scales[:], in_=wfc_grouped[:]
                )
            regroup_gated(s, 0, nc.vector.tensor_copy)

        last = ROUNDS - 1
        for n in range(last - ADD_LAG, last - 3):
            add_to_sum(n)
        regroup_gated(last - 1, 1, nc.scalar.copy)
        quantise_gated(last - 1)
        first_product(last, 0)
        second_product(last - 2)
        first_product(last, 1)
        second_product(last - 1, psum_flip, "flipped")
        gate(last)
        for a in range(TILES):
            regroup_gated(last, a, nc.vector.tensor_copy, P)
        for a in range(TILES):
            quantise_gated(last, a, 1)
        for n in range(last - 3, last):
            add_to_sum(n)
        sum_T_sb = keep.tile([P, F_CHUNKS, P], F32, name="sum_T_sb")
        nc.vector.tensor_copy(out=sum_T_sb[:], in_=sum_T[:])
        second_product(last)
        total_ps = psum_dist.tile([P, NF], F32, name="total_ps", tag="dist_bank")
        for c in range(F_CHUNKS):
            nc.tensor.transpose(total_ps[:, c * P : (c + 1) * P], sum_T_sb[:, c, :], ident_f32[:])
        total = keep.tile([P, NF], F32, name="total")
        halves = [slice(0, NF // 2), slice(NF // 2, NF)]
        late = [tanh_tiles[n][a] for n in (last - 1, last) for a in range(TILES)]
        terms = [late[1], late[2], total_ps, late[3]]
        for k in range(len(terms)):
            for half in halves:
                nc.vector.tensor_tensor(
                    out=total[:, half],
                    in0=terms[k][:, half],
                    in1=late[0][:, half] if k == 0 else total[:, half],
                    op=ALU.add,
                )
        out_rows = out.rearrange("b i f -> (b i) f")
        nc.sync.dma_start(out=out_rows[:, halves[0]], in_=total[:, halves[0]])
        nc.scalar.dma_start(out=out_rows[:, halves[1]], in_=total[:, halves[1]])
